import numpy as np
import ml_dtypes


def mxq(x, axis, fmt="e4m3"):
    dtype, down = {"e4m3": (ml_dtypes.float8_e4m3fn, 7), "e5m2": (ml_dtypes.float8_e5m2, 14)}[fmt]
    v = np.moveaxis(np.asarray(x, np.float32).astype(ml_dtypes.bfloat16).astype(np.float64), axis, -1)
    blocks = v.reshape(v.shape[:-1] + (-1, 32))
    amax = np.abs(blocks).max(-1, keepdims=True)
    byte = np.maximum(np.where(amax > 0, np.frexp(amax)[1] - 1 + 127, 0) - down, 1)
    scale = np.exp2(byte - 127.0)
    codes = (blocks / scale).astype(np.float32).astype(dtype).astype(np.float64)
    return np.moveaxis((codes * scale).reshape(v.shape), -1, axis)


WIDE = False


def mx_kscale(k):
    if not WIDE:
        return np.ones(k)
    levels = np.array([10, -10, 5, -5, 0])
    a = np.random.permutation(np.resize(levels, k // 512 * 4)).reshape(k // 512, 4)
    idx = np.arange(k)
    return np.exp2(a[idx // 512, idx % 128 // 32])


BF16 = ml_dtypes.bfloat16


def bf(x):
    return np.asarray(x, np.float32).astype(BF16)


def f64(x):
    return np.asarray(x).astype(np.float64)


B, DIM, D_IN, HID = 8192, 256, 128, 512
D_OUT = DIM - D_IN
LOG_SCALE_CLAMP = 2.0


def _net_draw(c_out):
    k, f = mx_kscale(HID), mx_kscale(HID)
    h = bf(np.maximum(np.random.standard_normal((B, HID)), 0.0) * np.sqrt(2.0) * k)
    w_hid = bf(np.random.standard_normal((HID, HID)) * np.sqrt(2.0 / HID) * f[:, None] / k[None, :])
    b_hid = bf(np.random.standard_normal(HID) * 0.3 * f)
    w_out = bf(np.random.standard_normal((D_OUT, HID)) * c_out / np.sqrt(HID) / f[None, :])
    b_out = bf(np.random.standard_normal(D_OUT) * 0.3)
    return h, w_hid, b_hid, w_out, b_out


def setup_inputs():
    z = bf(np.random.standard_normal((B, DIM)))
    h_s, s_Whid1, s_bhid1, s_Wout, s_bout = _net_draw(1.2)
    h_t, t_Whid1, t_bhid1, t_Wout, t_bout = _net_draw(1.0)
    return {"z": z, "h_s": h_s, "h_t": h_t,
            "s_Whid1": s_Whid1, "s_bhid1": s_bhid1, "s_Wout": s_Wout, "s_bout": s_bout,
            "t_Whid1": t_Whid1, "t_bhid1": t_bhid1, "t_Wout": t_Wout, "t_bout": t_bout}


def _tail(h, w_hid, b_hid, w_out, b_out):
    g = np.maximum((mxq(f64(h), 1, "e4m3") @ mxq(f64(w_hid), 1, "e4m3").T) + f64(b_hid), 0.0)
    return (mxq(g, 1, "e4m3") @ mxq(f64(w_out), 1, "e4m3").T) + f64(b_out)


def reference(z, h_s, h_t, s_Whid1, s_bhid1, s_Wout, s_bout, t_Whid1, t_bhid1, t_Wout, t_bout):
    z = f64(z)
    z1 = z[:, :D_IN]
    z2 = z[:, D_IN:]
    log_s = np.clip(_tail(h_s, s_Whid1, s_bhid1, s_Wout, s_bout), -LOG_SCALE_CLAMP, LOG_SCALE_CLAMP)
    t = _tail(h_t, t_Whid1, t_bhid1, t_Wout, t_bout)
    z2_out = z2 * np.exp(log_s) + t
    z_out = np.concatenate([z1, z2_out], axis=1)
    log_det = log_s.sum(axis=-1)
    return (z_out, log_det)

@@ -1,0 +1,294 @@
+from contextlib import ExitStack
+
+import concourse.mybir as mybir
+from concourse.masks import make_identity
+
+F32 = mybir.dt.float32
+BF16 = mybir.dt.bfloat16
+U32 = mybir.dt.uint32
+U8 = mybir.dt.uint8
+FP8X4 = mybir.dt.float8_e4m3fn_x4
+ACT = mybir.ActivationFunctionType
+ALU = mybir.AluOpType
+AX = mybir.AxisListType
+
+P = 128
+B, DIM, HID, D_OUT = 8192, 256, 512, 128
+ROWS_PP = B // P
+CH = 4
+SC = 8
+N_CHUNKS = ROWS_PP // CH
+N_UNITS = 2 * N_CHUNKS
+N_SC = ROWS_PP // SC
+FLOPS = 2 * 2 * B * HID * (HID + D_OUT)
+
+PIN = False
+H_ON_V = ()
+G_ON_V = ()
+Z1_ENGINE = "gpsimd"
+M_ENGINE = "gpsimd"
+
+
+def tile_affinecouplinglayer_pa_t_kernel(
+    tc, z, h_s, h_t, s_Whid1, s_bhid1, s_Wout, s_bout, t_Whid1, t_bhid1, t_Wout, t_bout, out_0, out_1
+):
+    nc = tc.nc
+    h_in = (h_s.rearrange("(p i) k -> p i k", i=ROWS_PP), h_t.rearrange("(p i) k -> p i k", i=ROWS_PP))
+    z_in = z.rearrange("(p i) d -> p i d", i=ROWS_PP)
+    zo = out_0.rearrange("(p i) d -> p i d", i=ROWS_PP)
+    w_hid = (s_Whid1, t_Whid1)
+    b_hid = (s_bhid1, t_bhid1)
+    w_out = (s_Wout, t_Wout)
+    b_out = (s_bout, t_bout)
+
+    with ExitStack() as ctx:
+        const = ctx.enter_context(tc.tile_pool(name="const", bufs=1))
+        hpool = ctx.enter_context(tc.tile_pool(name="hpool", bufs=3))
+        zpool = ctx.enter_context(tc.tile_pool(name="zpool", bufs=4))
+        work = ctx.enter_context(tc.tile_pool(name="work", bufs=3))
+        epi = ctx.enter_context(tc.tile_pool(name="epi", bufs=3))
+        tp_pool = ctx.enter_context(tc.psum_pool(name="tp_pool", bufs=2))
+        m1_pool = ctx.enter_context(tc.psum_pool(name="m1_pool", bufs=4))
+        m2_pool = ctx.enter_context(tc.psum_pool(name="m2_pool", bufs=2))
+        if PIN:
+            ctx.enter_context(tc.manual_schedule())
+
+        w_sb = []
+        wo_sb = []
+        bh_raw = []
+        bo_raw = []
+        h_sb = {}
+        z_sb = {}
+
+        def load_h(n, s, pieces):
+            t = hpool.tile([P, SC * HID], BF16, name="h%d" % n)
+            h_sb[(n, s)] = t
+            step = SC // pieces
+            for q in range(pieces):
+                nc.sync.dma_start(
+                    out=t[:, q * step * HID : (q + 1) * step * HID].rearrange("p (i k) -> p i k", k=HID),
+                    in_=h_in[n][:, s * SC + q * step : s * SC + (q + 1) * step, :],
+                )
+
+        def load_z(s):
+            t = zpool.tile([P, SC, DIM], BF16, name="zt")
+            z_sb[s] = t
+            nc.sync.dma_start(out=t[:], in_=z_in[:, s * SC : (s + 1) * SC, :])
+
+        for n in range(2):
+            wt = const.tile([P, 4 * HID], BF16, name="w_sb%d" % n)
+            nc.sync.dma_start(out=wt[:], in_=w_hid[n].rearrange("(p t) k -> p (t k)", t=4))
+            w_sb.append(wt)
+            load_h(n, 0, 2)
+            br = const.tile([P, 4], BF16, name="bh_raw%d" % n)
+            nc.scalar.dma_start(out=br[:], in_=b_hid[n].rearrange("(p t) -> p t", t=4))
+            bh_raw.append(br)
+            wo = const.tile([P, HID], BF16, name="wo_sb%d" % n)
+            nc.scalar.dma_start(out=wo[:], in_=w_out[n])
+            wo_sb.append(wo)
+        for n in range(2):
+            bo = const.tile([P, D_OUT], BF16, name="bo_raw%d" % n)
+            nc.scalar.dma_start(out=bo[:], in_=b_out[n].partition_broadcast(P))
+            bo_raw.append(bo)
+        load_z(0)
+        for n in range(2):
+            load_h(n, 1, 1)
+        load_z(1)
+
+        ident = const.tile([P, P], F32, name="ident")
+        make_identity(nc, ident[:])
+
+        counters = {"h": 0, "g": 0}
+
+        def copy_out(out, in_):
+            i = counters["h"] % 4
+            counters["h"] += 1
+            if i in H_ON_V:
+                nc.vector.tensor_copy(out=out, in_=in_)
+            else:
+                nc.scalar.copy(out=out, in_=in_)
+
+        def to_k_major(words, first_word, grouped):
+            gw = grouped[:].bitcast(F32)
+            for half in range(2):
+                bank = tp_pool.tile([P, 2, 256], F32, name="tp")
+                for r2 in range(2):
+                    for uu in range(2):
+                        w0 = first_word + (2 * half + r2) * 256 + uu * P
+                        nc.tensor.transpose(bank[:, uu, r2 * P : (r2 + 1) * P], words[:, w0 : w0 + P], ident[:])
+                copy_out(
+                    gw[:, half * 512 : (half + 1) * 512].rearrange("p (b u) -> p b u", u=2),
+                    bank[:].rearrange("p u b -> p b u"),
+                )
+
+        wc, wsc, woc, wosc, bh, bo = [], [], [], [], [], []
+        def prep_w(n):
+            wq = work.tile([P, 4 * HID], BF16, name="hq", align_bytes=64)
+            to_k_major(w_sb[n][:].bitcast(F32), 0, wq)
+            c = const.tile([P, HID], U32, name="wc%d" % n, align_bytes=64)
+            s = const.tile([P, HID], U8, name="wsc%d" % n, align_bytes=64)
+            nc.vector.quantize_mx(out=c[:].bitcast(FP8X4), scales=s[:], in_=wq[:])
+            wc.append(c)
+            wsc.append(s)
+            b32 = const.tile([P, 4], F32, name="bh%d" % n)
+            nc.vector.tensor_copy(out=b32[:], in_=bh_raw[n][:])
+            bh.append(b32)
+
+        def prep_wout(n):
+            bank = tp_pool.tile([P, 2, 256], F32, name="tp")
+            wv = wo_sb[n][:].bitcast(F32).rearrange("p (q u) -> p u q", u=2)
+            for uu in range(2):
+                nc.tensor.transpose(bank[:, uu, 0:P], wv[:, uu, :], ident[:])
+            woq = const.tile([P, 4 * D_OUT], BF16, name="woq%d" % n, align_bytes=64)
+            nc.vector.tensor_copy(
+                out=woq[:].bitcast(F32).rearrange("p (b u) -> p b u", u=2),
+                in_=bank[:, :, 0:P].rearrange("p u b -> p b u"),
+            )
+            c = const.tile([P, D_OUT], U32, name="woc%d" % n, align_bytes=64)
+            s = const.tile([P, D_OUT], U8, name="wosc%d" % n, align_bytes=64)
+            nc.vector.quantize_mx(out=c[:].bitcast(FP8X4), scales=s[:], in_=woq[:])
+            woc.append(c)
+            wosc.append(s)
+            b32 = const.tile([P, D_OUT], F32, name="bo%d" % n)
+            nc.vector.tensor_copy(out=b32[:], in_=bo_raw[n][:])
+            bo.append(b32)
+
+        ld = const.tile([P, ROWS_PP], F32, name="ld")
+
+        hq, hc, hsc, gt, gg, gc, gsc, o_ps = {}, {}, {}, {}, {}, {}, {}, {}
+        ls_t, ex_t, sh_t, ot_t = {}, {}, {}, {}
+
+        def stage_a(u):
+            c, n = u // 2, u % 2
+            t = work.tile([P, 4 * HID], BF16, name="hq", align_bytes=64)
+            hq[u] = t
+            to_k_major(h_sb[(n, c // 2)][:].bitcast(F32), (c % 2) * CH * 256, t)
+
+        def stage_b(u):
+            c = work.tile([P, HID], U32, name="hc", align_bytes=64)
+            s = work.tile([P, HID], U8, name="hsc", align_bytes=64)
+            nc.vector.quantize_mx(out=c[:].bitcast(FP8X4), scales=s[:], in_=hq[u][:])
+            hc[u], hsc[u] = c, s
+
+        def stage_c(u):
+            n = u % 2
+            g = work.tile([P, 4, 512], BF16, name="gt")
+            gt[u] = g
+            for t in range(4):
+                acc = m1_pool.tile([P, 512], F32, name="m1")
+                nc.tensor.matmul_mx(
+                    out=acc[:],
+                    lhsT=wc[n][:, t * P : (t + 1) * P].bitcast(FP8X4),
+                    lhsT_scale=wsc[n][:, t * P : (t + 1) * P],
+                    rhs=hc[u][:].bitcast(FP8X4),
+                    rhs_scale=hsc[u][:],
+                    start=True,
+                    stop=True,
+                )
+                i = counters["g"] % 8
+                counters["g"] += 1
+                if i in G_ON_V:
+                    nc.vector.tensor_scalar(
+                        out=g[:, t, :], in0=acc[:], scalar1=bh[n][:, t : t + 1], scalar2=0.0, op0=ALU.add, op1=ALU.max
+                    )
+                else:
+                    nc.scalar.activation(out=g[:, t, :], in_=acc[:], func=ACT.Relu, bias=bh[n][:, t : t + 1], scale=1.0)
+
+        def stage_d(u):
+            t = work.tile([P, 512, 4], BF16, name="gg", align_bytes=64)
+            gg[u] = t
+            nc.vector.tensor_copy(
+                out=t[:].rearrange("p (c i) t -> p c t i", i=4),
+                in_=gt[u][:].rearrange("p t (c i) -> p c t i", i=4),
+            )
+
+        def stage_e(u):
+            c = work.tile([P, HID], U32, name="gc", align_bytes=64)
+            s = work.tile([P, HID], U8, name="gsc", align_bytes=64)
+            nc.vector.quantize_mx(out=c[:].bitcast(FP8X4), scales=s[:], in_=gg[u][:].rearrange("p b t -> p (b t)"))
+            gc[u], gsc[u] = c, s
+
+        def stage_f(u):
+            n = u % 2
+            o = m2_pool.tile([P, CH, D_OUT], F32, name="m2")
+            o_ps[u] = o
+            for r in range(CH):
+                nc.tensor.matmul_mx(
+                    out=o[:, r, :],
+                    lhsT=gc[u][:, r * P : (r + 1) * P].bitcast(FP8X4),
+                    lhsT_scale=gsc[u][:, r * P : (r + 1) * P],
+                    rhs=woc[n][:].bitcast(FP8X4),
+                    rhs_scale=wosc[n][:],
+                    start=True,
+                    stop=True,
+                )
+
+        def bias_rows(n):
+            return bo[n][:].unsqueeze(1).to_broadcast([P, CH, D_OUT])
+
+        def z_rows(c, lo):
+            i0 = (c % 2) * CH
+            return z_sb[c // 2][:, i0 : i0 + CH, lo : lo + D_OUT]
+
+        def epi_1(c):
+            ls = epi.tile([P, CH, D_OUT], F32, name="ls")
+            ls_t[c] = ls
+            nc.vector.tensor_tensor(out=ls[:], in0=o_ps[2 * c][:], in1=bias_rows(0), op=ALU.add)
+            nc.vector.tensor_scalar(out=ls[:], in0=ls[:], scalar1=-2.0, scalar2=2.0, op0=ALU.max, op1=ALU.min)
+            nc.vector.tensor_reduce(out=ld[:, c * CH : (c + 1) * CH], in_=ls[:], axis=AX.X, op=ALU.add)
+            sh = epi.tile([P, CH, D_OUT], F32, name="sh")
+            sh_t[c] = sh
+            nc.vector.tensor_tensor(out=sh[:], in0=o_ps[2 * c + 1][:], in1=bias_rows(1), op=ALU.add)
+            ot = epi.tile([P, CH, DIM], F32, name="ot")
+            ot_t[c] = ot
+            if Z1_ENGINE == "gpsimd":
+                nc.gpsimd.tensor_scalar(
+                    out=ot[:, :, 0:D_OUT], in0=z_rows(c, 0), scalar1=1.0, scalar2=0.0, op0=ALU.mult, op1=ALU.add
+                )
+            else:
+                nc.vector.tensor_copy(out=ot[:, :, 0:D_OUT], in_=z_rows(c, 0))
+
+        def epi_2(c):
+            ex = epi.tile([P, CH, D_OUT], F32, name="ex")
+            ex_t[c] = ex
+            nc.scalar.activation(out=ex[:], in_=ls_t[c][:], func=ACT.Exp)
+
+        def epi_3(c):
+            ex = ex_t[c]
+            eng = nc.gpsimd if M_ENGINE == "gpsimd" else nc.vector
+            eng.tensor_tensor(out=ex[:], in0=z_rows(c, D_OUT), in1=ex[:], op=ALU.mult)
+            nc.vector.tensor_tensor(out=ot_t[c][:, :, D_OUT:DIM], in0=ex[:], in1=sh_t[c][:], op=ALU.add)
+            nc.sync.dma_start(out=zo[:, c * CH : (c + 1) * CH, :], in_=ot_t[c][:])
+
+        prep_w(0)
+        stage_a(0)
+        stage_b(0)
+        prep_w(1)
+        stage_a(1)
+        prep_wout(0)
+        prep_wout(1)
+        for it in range(N_UNITS + 5):
+            if it + 2 < N_UNITS:
+                if (it + 2) % 4 == 0:
+                    s_next = (it + 2) // 4 + 1
+                    if s_next < N_SC:
+                        for n in range(2):
+                            load_h(n, s_next, 1)
+                        load_z(s_next)
+                stage_a(it + 2)
+            if it < N_UNITS:
+                stage_c(it)
+            if it >= 4 and it % 2 == 0 and (it - 4) // 2 < N_CHUNKS:
+                epi_3((it - 4) // 2)
+            if it >= 3 and it % 2 == 1 and (it - 3) // 2 < N_CHUNKS:
+                epi_1((it - 3) // 2)
+            if 0 <= it - 1 < N_UNITS:
+                stage_d(it - 1)
+            if it + 1 < N_UNITS:
+                stage_b(it + 1)
+            if 0 <= it - 1 < N_UNITS:
+                stage_e(it - 1)
+                stage_f(it - 1)
+            if it >= 3 and it % 2 == 1 and (it - 3) // 2 < N_CHUNKS:
+                epi_2((it - 3) // 2)
+        nc.sync.dma_start(out=out_1.rearrange("(p i) -> p i", i=ROWS_PP), in_=ld[:])

@@ -22,11 +22,11 @@ N_UNITS = 2 * N_CHUNKS
 N_SC = ROWS_PP // SC
 FLOPS = 2 * 2 * B * HID * (HID + D_OUT)
 
-PIN = False
+PIN = True
 H_ON_V = ()
 G_ON_V = ()
-Z1_ENGINE = "gpsimd"
-M_ENGINE = "gpsimd"
+Z1_ENGINE = "scalar"
+M_ENGINE = "vector"
 
 
 def tile_affinecouplinglayer_pa_t_kernel(
@@ -60,15 +60,16 @@ def tile_affinecouplinglayer_pa_t_kernel(
         h_sb = {}
         z_sb = {}
 
-        def load_h(n, s, pieces):
+        def load_h_rows(n, s, i0, i1):
+            nc.sync.dma_start(
+                out=h_sb[(n, s)][:, i0 * HID : i1 * HID].rearrange("p (i k) -> p i k", k=HID),
+                in_=h_in[n][:, s * SC + i0 : s * SC + i1, :],
+            )
+
+        def load_h(n, s):
             t = hpool.tile([P, SC * HID], BF16, name="h%d" % n)
             h_sb[(n, s)] = t
-            step = SC // pieces
-            for q in range(pieces):
-                nc.sync.dma_start(
-                    out=t[:, q * step * HID : (q + 1) * step * HID].rearrange("p (i k) -> p i k", k=HID),
-                    in_=h_in[n][:, s * SC + q * step : s * SC + (q + 1) * step, :],
-                )
+            load_h_rows(n, s, 0, SC)
 
         def load_z(s):
             t = zpool.tile([P, SC, DIM], BF16, name="zt")
@@ -79,7 +80,9 @@ def tile_affinecouplinglayer_pa_t_kernel(
             wt = const.tile([P, 4 * HID], BF16, name="w_sb%d" % n)
             nc.sync.dma_start(out=wt[:], in_=w_hid[n].rearrange("(p t) k -> p (t k)", t=4))
             w_sb.append(wt)
-            load_h(n, 0, 2)
+            h0 = hpool.tile([P, SC * HID], BF16, name="h%d" % n)
+            h_sb[(n, 0)] = h0
+            load_h_rows(n, 0, 0, CH)
             br = const.tile([P, 4], BF16, name="bh_raw%d" % n)
             nc.scalar.dma_start(out=br[:], in_=b_hid[n].rearrange("(p t) -> p t", t=4))
             bh_raw.append(br)
@@ -90,9 +93,11 @@ def tile_affinecouplinglayer_pa_t_kernel(
             bo = const.tile([P, D_OUT], BF16, name="bo_raw%d" % n)
             nc.scalar.dma_start(out=bo[:], in_=b_out[n].partition_broadcast(P))
             bo_raw.append(bo)
+        for n in range(2):
+            load_h_rows(n, 0, CH, SC)
         load_z(0)
         for n in range(2):
-            load_h(n, 1, 1)
+            load_h(n, 1)
         load_z(1)
 
         ident = const.tile([P, P], F32, name="ident")
@@ -100,18 +105,21 @@ def tile_affinecouplinglayer_pa_t_kernel(
 
         counters = {"h": 0, "g": 0}
 
-        def copy_out(out, in_):
+        def copy_out(out, in_, on_vector):
             i = counters["h"] % 4
             counters["h"] += 1
-            if i in H_ON_V:
+            if on_vector or i in H_ON_V:
                 nc.vector.tensor_copy(out=out, in_=in_)
             else:
                 nc.scalar.copy(out=out, in_=in_)
 
-        def to_k_major(words, first_word, grouped):
+        def to_k_major(words, first_word, grouped, prologue=False):
             gw = grouped[:].bitcast(F32)
             for half in range(2):
-                bank = tp_pool.tile([P, 2, 256], F32, name="tp")
+                if prologue:
+                    bank = m1_pool.tile([P, 2, 256], F32, name="m1")
+                else:
+                    bank = tp_pool.tile([P, 2, 256], F32, name="tp")
                 for r2 in range(2):
                     for uu in range(2):
                         w0 = first_word + (2 * half + r2) * 256 + uu * P
@@ -119,12 +127,13 @@ def tile_affinecouplinglayer_pa_t_kernel(
                 copy_out(
                     gw[:, half * 512 : (half + 1) * 512].rearrange("p (b u) -> p b u", u=2),
                     bank[:].rearrange("p u b -> p b u"),
+                    prologue,
                 )
 
         wc, wsc, woc, wosc, bh, bo = [], [], [], [], [], []
         def prep_w(n):
             wq = work.tile([P, 4 * HID], BF16, name="hq", align_bytes=64)
-            to_k_major(w_sb[n][:].bitcast(F32), 0, wq)
+            to_k_major(w_sb[n][:].bitcast(F32), 0, wq, True)
             c = const.tile([P, HID], U32, name="wc%d" % n, align_bytes=64)
             s = const.tile([P, HID], U8, name="wsc%d" % n, align_bytes=64)
             nc.vector.quantize_mx(out=c[:].bitcast(FP8X4), scales=s[:], in_=wq[:])
@@ -135,7 +144,7 @@ def tile_affinecouplinglayer_pa_t_kernel(
             bh.append(b32)
 
         def prep_wout(n):
-            bank = tp_pool.tile([P, 2, 256], F32, name="tp")
+            bank = m2_pool.tile([P, 2, 256], F32, name="m2")
             wv = wo_sb[n][:].bitcast(F32).rearrange("p (q u) -> p u q", u=2)
             for uu in range(2):
                 nc.tensor.transpose(bank[:, uu, 0:P], wv[:, uu, :], ident[:])
@@ -156,7 +165,7 @@ def tile_affinecouplinglayer_pa_t_kernel(
         ld = const.tile([P, ROWS_PP], F32, name="ld")
 
         hq, hc, hsc, gt, gg, gc, gsc, o_ps = {}, {}, {}, {}, {}, {}, {}, {}
-        ls_t, ex_t, sh_t, ot_t = {}, {}, {}, {}
+        ls_t, ex_t, ot_t = {}, {}, {}
 
         def stage_a(u):
             c, n = u // 2, u % 2
@@ -230,34 +239,30 @@ def tile_affinecouplinglayer_pa_t_kernel(
             i0 = (c % 2) * CH
             return z_sb[c // 2][:, i0 : i0 + CH, lo : lo + D_OUT]
 
-        def epi_1(c):
+        def epi_a(c):
             ls = epi.tile([P, CH, D_OUT], F32, name="ls")
             ls_t[c] = ls
             nc.vector.tensor_tensor(out=ls[:], in0=o_ps[2 * c][:], in1=bias_rows(0), op=ALU.add)
             nc.vector.tensor_scalar(out=ls[:], in0=ls[:], scalar1=-2.0, scalar2=2.0, op0=ALU.max, op1=ALU.min)
             nc.vector.tensor_reduce(out=ld[:, c * CH : (c + 1) * CH], in_=ls[:], axis=AX.X, op=ALU.add)
-            sh = epi.tile([P, CH, D_OUT], F32, name="sh")
-            sh_t[c] = sh
-            nc.vector.tensor_tensor(out=sh[:], in0=o_ps[2 * c + 1][:], in1=bias_rows(1), op=ALU.add)
             ot = epi.tile([P, CH, DIM], F32, name="ot")
             ot_t[c] = ot
-            if Z1_ENGINE == "gpsimd":
-                nc.gpsimd.tensor_scalar(
-                    out=ot[:, :, 0:D_OUT], in0=z_rows(c, 0), scalar1=1.0, scalar2=0.0, op0=ALU.mult, op1=ALU.add
-                )
+            if Z1_ENGINE == "scalar":
+                nc.scalar.copy(out=ot[:, :, 0:D_OUT], in_=z_rows(c, 0))
             else:
                 nc.vector.tensor_copy(out=ot[:, :, 0:D_OUT], in_=z_rows(c, 0))
 
-        def epi_2(c):
+        def epi_exp(c):
             ex = epi.tile([P, CH, D_OUT], F32, name="ex")
             ex_t[c] = ex
             nc.scalar.activation(out=ex[:], in_=ls_t[c][:], func=ACT.Exp)
 
-        def epi_3(c):
+        def epi_b(c):
+            sh = epi.tile([P, CH, D_OUT], F32, name="sh")
+            nc.vector.tensor_tensor(out=sh[:], in0=o_ps[2 * c + 1][:], in1=bias_rows(1), op=ALU.add)
             ex = ex_t[c]
-            eng = nc.gpsimd if M_ENGINE == "gpsimd" else nc.vector
-            eng.tensor_tensor(out=ex[:], in0=z_rows(c, D_OUT), in1=ex[:], op=ALU.mult)
-            nc.vector.tensor_tensor(out=ot_t[c][:, :, D_OUT:DIM], in0=ex[:], in1=sh_t[c][:], op=ALU.add)
+            nc.vector.tensor_tensor(out=ex[:], in0=z_rows(c, D_OUT), in1=ex[:], op=ALU.mult)
+            nc.vector.tensor_tensor(out=ot_t[c][:, :, D_OUT:DIM], in0=ex[:], in1=sh[:], op=ALU.add)
             nc.sync.dma_start(out=zo[:, c * CH : (c + 1) * CH, :], in_=ot_t[c][:])
 
         prep_w(0)
@@ -267,21 +272,21 @@ def tile_affinecouplinglayer_pa_t_kernel(
         stage_a(1)
         prep_wout(0)
         prep_wout(1)
-        for it in range(N_UNITS + 5):
+        for it in range(N_UNITS + 4):
+            c_a = (it - 2) // 2 if (it >= 2 and it % 2 == 0) else -1
+            c_b = (it - 3) // 2 if (it >= 3 and it % 2 == 1) else -1
+            if 0 <= c_b < N_CHUNKS:
+                epi_exp(c_b)
+            if it < N_UNITS:
+                stage_c(it)
             if it + 2 < N_UNITS:
                 if (it + 2) % 4 == 0:
                     s_next = (it + 2) // 4 + 1
                     if s_next < N_SC:
                         for n in range(2):
-                            load_h(n, s_next, 1)
+                            load_h(n, s_next)
                         load_z(s_next)
                 stage_a(it + 2)
-            if it < N_UNITS:
-                stage_c(it)
-            if it >= 4 and it % 2 == 0 and (it - 4) // 2 < N_CHUNKS:
-                epi_3((it - 4) // 2)
-            if it >= 3 and it % 2 == 1 and (it - 3) // 2 < N_CHUNKS:
-                epi_1((it - 3) // 2)
             if 0 <= it - 1 < N_UNITS:
                 stage_d(it - 1)
             if it + 1 < N_UNITS:
@@ -289,6 +294,8 @@ def tile_affinecouplinglayer_pa_t_kernel(
             if 0 <= it - 1 < N_UNITS:
                 stage_e(it - 1)
                 stage_f(it - 1)
-            if it >= 3 and it % 2 == 1 and (it - 3) // 2 < N_CHUNKS:
-                epi_2((it - 3) // 2)
+            if 0 <= c_a < N_CHUNKS:
+                epi_a(c_a)
+            if 0 <= c_b < N_CHUNKS:
+                epi_b(c_b)
         nc.sync.dma_start(out=out_1.rearrange("(p i) -> p i", i=ROWS_PP), in_=ld[:])

@@ -22,7 +22,7 @@ N_UNITS = 2 * N_CHUNKS
 N_SC = ROWS_PP // SC
 FLOPS = 2 * 2 * B * HID * (HID + D_OUT)
 
-PIN = True
+PIN = False
 H_ON_V = ()
 G_ON_V = ()
 Z1_ENGINE = "scalar"
@@ -45,8 +45,8 @@ def tile_affinecouplinglayer_pa_t_kernel(
         const = ctx.enter_context(tc.tile_pool(name="const", bufs=1))
         hpool = ctx.enter_context(tc.tile_pool(name="hpool", bufs=3))
         zpool = ctx.enter_context(tc.tile_pool(name="zpool", bufs=4))
-        work = ctx.enter_context(tc.tile_pool(name="work", bufs=3))
-        epi = ctx.enter_context(tc.tile_pool(name="epi", bufs=3))
+        work = ctx.enter_context(tc.tile_pool(name="work", bufs=4))
+        epi = ctx.enter_context(tc.tile_pool(name="epi", bufs=4))
         tp_pool = ctx.enter_context(tc.psum_pool(name="tp_pool", bufs=2))
         m1_pool = ctx.enter_context(tc.psum_pool(name="m1_pool", bufs=4))
         m2_pool = ctx.enter_context(tc.psum_pool(name="m2_pool", bufs=2))
@@ -165,7 +165,7 @@ def tile_affinecouplinglayer_pa_t_kernel(
         ld = const.tile([P, ROWS_PP], F32, name="ld")
 
         hq, hc, hsc, gt, gg, gc, gsc, o_ps = {}, {}, {}, {}, {}, {}, {}, {}
-        ls_t, ex_t, ot_t = {}, {}, {}
+        ls_t, ex_t, ot_t, sh_t = {}, {}, {}, {}
 
         def stage_a(u):
             c, n = u // 2, u % 2
@@ -245,24 +245,26 @@ def tile_affinecouplinglayer_pa_t_kernel(
             nc.vector.tensor_tensor(out=ls[:], in0=o_ps[2 * c][:], in1=bias_rows(0), op=ALU.add)
             nc.vector.tensor_scalar(out=ls[:], in0=ls[:], scalar1=-2.0, scalar2=2.0, op0=ALU.max, op1=ALU.min)
             nc.vector.tensor_reduce(out=ld[:, c * CH : (c + 1) * CH], in_=ls[:], axis=AX.X, op=ALU.add)
+
+        def epi_z1(c):
             ot = epi.tile([P, CH, DIM], F32, name="ot")
             ot_t[c] = ot
-            if Z1_ENGINE == "scalar":
-                nc.scalar.copy(out=ot[:, :, 0:D_OUT], in_=z_rows(c, 0))
-            else:
-                nc.vector.tensor_copy(out=ot[:, :, 0:D_OUT], in_=z_rows(c, 0))
+            nc.scalar.copy(out=ot[:, :, 0:D_OUT], in_=z_rows(c, 0))
 
         def epi_exp(c):
             ex = epi.tile([P, CH, D_OUT], F32, name="ex")
             ex_t[c] = ex
             nc.scalar.activation(out=ex[:], in_=ls_t[c][:], func=ACT.Exp)
 
-        def epi_b(c):
+        def epi_sh(c):
             sh = epi.tile([P, CH, D_OUT], F32, name="sh")
+            sh_t[c] = sh
             nc.vector.tensor_tensor(out=sh[:], in0=o_ps[2 * c + 1][:], in1=bias_rows(1), op=ALU.add)
+
+        def epi_out(c):
             ex = ex_t[c]
             nc.vector.tensor_tensor(out=ex[:], in0=z_rows(c, D_OUT), in1=ex[:], op=ALU.mult)
-            nc.vector.tensor_tensor(out=ot_t[c][:, :, D_OUT:DIM], in0=ex[:], in1=sh[:], op=ALU.add)
+            nc.vector.tensor_tensor(out=ot_t[c][:, :, D_OUT:DIM], in0=ex[:], in1=sh_t[c][:], op=ALU.add)
             nc.sync.dma_start(out=zo[:, c * CH : (c + 1) * CH, :], in_=ot_t[c][:])
 
         prep_w(0)
@@ -272,30 +274,39 @@ def tile_affinecouplinglayer_pa_t_kernel(
         stage_a(1)
         prep_wout(0)
         prep_wout(1)
-        for it in range(N_UNITS + 4):
-            c_a = (it - 2) // 2 if (it >= 2 and it % 2 == 0) else -1
-            c_b = (it - 3) // 2 if (it >= 3 and it % 2 == 1) else -1
-            if 0 <= c_b < N_CHUNKS:
-                epi_exp(c_b)
+        stage_a(2)
+
+        def chunk_at(it, first):
+            c = (it - first) // 2
+            return c if (it >= first and (it - first) % 2 == 0 and c < N_CHUNKS) else -1
+
+        for it in range(N_UNITS + 7):
             if it < N_UNITS:
                 stage_c(it)
-            if it + 2 < N_UNITS:
-                if (it + 2) % 4 == 0:
-                    s_next = (it + 2) // 4 + 1
+            if it + 3 < N_UNITS:
+                if (it + 3) % 4 == 0:
+                    s_next = (it + 3) // 4 + 1
                     if s_next < N_SC:
                         for n in range(2):
                             load_h(n, s_next)
                         load_z(s_next)
-                stage_a(it + 2)
-            if 0 <= it - 1 < N_UNITS:
-                stage_d(it - 1)
+                stage_a(it + 3)
+            if 0 <= it - 2 < N_UNITS:
+                stage_f(it - 2)
+            if chunk_at(it, 3) >= 0:
+                epi_z1(chunk_at(it, 3))
+            if chunk_at(it, 4) >= 0:
+                epi_exp(chunk_at(it, 4))
             if it + 1 < N_UNITS:
                 stage_b(it + 1)
             if 0 <= it - 1 < N_UNITS:
+                stage_d(it - 1)
+            if chunk_at(it, 3) >= 0:
+                epi_a(chunk_at(it, 3))
+            if chunk_at(it, 4) >= 0:
+                epi_sh(chunk_at(it, 4))
+            if chunk_at(it, 6) >= 0:
+                epi_out(chunk_at(it, 6))
+            if 0 <= it - 1 < N_UNITS:
                 stage_e(it - 1)
-                stage_f(it - 1)
-            if 0 <= c_a < N_CHUNKS:
-                epi_a(c_a)
-            if 0 <= c_b < N_CHUNKS:
-                epi_b(c_b)
         nc.sync.dma_start(out=out_1.rearrange("(p i) -> p i", i=ROWS_PP), in_=ld[:])

@@ -22,11 +22,11 @@ N_UNITS = 2 * N_CHUNKS
 N_SC = ROWS_PP // SC
 FLOPS = 2 * 2 * B * HID * (HID + D_OUT)
 
-PIN = False
+PIN = True
 H_ON_V = ()
 G_ON_V = ()
-Z1_ENGINE = "scalar"
-M_ENGINE = "vector"
+Z1_ENGINE = "gpsimd"
+M_ENGINE = "gpsimd"
 
 
 def tile_affinecouplinglayer_pa_t_kernel(
@@ -44,7 +44,8 @@ def tile_affinecouplinglayer_pa_t_kernel(
     with ExitStack() as ctx:
         const = ctx.enter_context(tc.tile_pool(name="const", bufs=1))
         hpool = ctx.enter_context(tc.tile_pool(name="hpool", bufs=3))
-        zpool = ctx.enter_context(tc.tile_pool(name="zpool", bufs=4))
+        zpool = ctx.enter_context(tc.tile_pool(name="zpool", bufs=5))
+        gate = ctx.enter_context(tc.tile_pool(name="gate", bufs=1))
         work = ctx.enter_context(tc.tile_pool(name="work", bufs=4))
         epi = ctx.enter_context(tc.tile_pool(name="epi", bufs=4))
         tp_pool = ctx.enter_context(tc.psum_pool(name="tp_pool", bufs=2))
@@ -165,7 +166,7 @@ def tile_affinecouplinglayer_pa_t_kernel(
         ld = const.tile([P, ROWS_PP], F32, name="ld")
 
         hq, hc, hsc, gt, gg, gc, gsc, o_ps = {}, {}, {}, {}, {}, {}, {}, {}
-        ls_t, ex_t, ot_t, sh_t = {}, {}, {}, {}
+        ls_t, ex_t, ot_t, sh_t, mz_t = {}, {}, {}, {}, {}
 
         def stage_a(u):
             c, n = u // 2, u % 2
@@ -239,17 +240,27 @@ def tile_affinecouplinglayer_pa_t_kernel(
             i0 = (c % 2) * CH
             return z_sb[c // 2][:, i0 : i0 + CH, lo : lo + D_OUT]
 
-        def epi_a(c):
+        def epi_a1(c):
             ls = epi.tile([P, CH, D_OUT], F32, name="ls")
             ls_t[c] = ls
             nc.vector.tensor_tensor(out=ls[:], in0=o_ps[2 * c][:], in1=bias_rows(0), op=ALU.add)
+
+        def epi_clamp(c):
+            ls = ls_t[c]
             nc.vector.tensor_scalar(out=ls[:], in0=ls[:], scalar1=-2.0, scalar2=2.0, op0=ALU.max, op1=ALU.min)
-            nc.vector.tensor_reduce(out=ld[:, c * CH : (c + 1) * CH], in_=ls[:], axis=AX.X, op=ALU.add)
+
+        def epi_sum(c):
+            nc.vector.tensor_reduce(out=ld[:, c * CH : (c + 1) * CH], in_=ls_t[c][:], axis=AX.X, op=ALU.add)
 
         def epi_z1(c):
             ot = epi.tile([P, CH, DIM], F32, name="ot")
             ot_t[c] = ot
-            nc.scalar.copy(out=ot[:, :, 0:D_OUT], in_=z_rows(c, 0))
+            if Z1_ENGINE == "gpsimd":
+                nc.gpsimd.tensor_scalar(
+                    out=ot[:, :, 0:D_OUT], in0=z_rows(c, 0), scalar1=1.0, scalar2=0.0, op0=ALU.mult, op1=ALU.add
+                )
+            else:
+                nc.scalar.copy(out=ot[:, :, 0:D_OUT], in_=z_rows(c, 0))
 
         def epi_exp(c):
             ex = epi.tile([P, CH, D_OUT], F32, name="ex")
@@ -261,10 +272,14 @@ def tile_affinecouplinglayer_pa_t_kernel(
             sh_t[c] = sh
             nc.vector.tensor_tensor(out=sh[:], in0=o_ps[2 * c + 1][:], in1=bias_rows(1), op=ALU.add)
 
+        def epi_m(c):
+            mz = gate.tile([P, CH, D_OUT], F32, name="mz")
+            mz_t[c] = mz
+            eng = nc.gpsimd if M_ENGINE == "gpsimd" else nc.vector
+            eng.tensor_tensor(out=mz[:], in0=z_rows(c, D_OUT), in1=ex_t[c][:], op=ALU.mult)
+
         def epi_out(c):
-            ex = ex_t[c]
-            nc.vector.tensor_tensor(out=ex[:], in0=z_rows(c, D_OUT), in1=ex[:], op=ALU.mult)
-            nc.vector.tensor_tensor(out=ot_t[c][:, :, D_OUT:DIM], in0=ex[:], in1=sh_t[c][:], op=ALU.add)
+            nc.vector.tensor_tensor(out=ot_t[c][:, :, D_OUT:DIM], in0=mz_t[c][:], in1=sh_t[c][:], op=ALU.add)
             nc.sync.dma_start(out=zo[:, c * CH : (c + 1) * CH, :], in_=ot_t[c][:])
 
         prep_w(0)
@@ -272,17 +287,23 @@ def tile_affinecouplinglayer_pa_t_kernel(
         stage_b(0)
         prep_w(1)
         stage_a(1)
-        prep_wout(0)
-        prep_wout(1)
         stage_a(2)
 
         def chunk_at(it, first):
             c = (it - first) // 2
             return c if (it >= first and (it - first) % 2 == 0 and c < N_CHUNKS) else -1
 
+        def when(it, first, fn):
+            c = chunk_at(it, first)
+            if c >= 0:
+                fn(c)
+
         for it in range(N_UNITS + 7):
             if it < N_UNITS:
                 stage_c(it)
+            if it == 0:
+                prep_wout(0)
+                prep_wout(1)
             if it + 3 < N_UNITS:
                 if (it + 3) % 4 == 0:
                     s_next = (it + 3) // 4 + 1
@@ -291,22 +312,25 @@ def tile_affinecouplinglayer_pa_t_kernel(
                             load_h(n, s_next)
                         load_z(s_next)
                 stage_a(it + 3)
-            if 0 <= it - 2 < N_UNITS:
-                stage_f(it - 2)
-            if chunk_at(it, 3) >= 0:
-                epi_z1(chunk_at(it, 3))
-            if chunk_at(it, 4) >= 0:
-                epi_exp(chunk_at(it, 4))
+            c_f = chunk_at(it, 3)
+            if c_f >= 0:
+                stage_f(2 * c_f)
+                stage_f(2 * c_f + 1)
+            if 0 <= it - 1 < N_UNITS:
+                stage_d(it - 1)
+            when(it, 5, epi_clamp)
+            if M_ENGINE != "gpsimd":
+                when(it, 7, epi_m)
             if it + 1 < N_UNITS:
                 stage_b(it + 1)
             if 0 <= it - 1 < N_UNITS:
-                stage_d(it - 1)
-            if chunk_at(it, 3) >= 0:
-                epi_a(chunk_at(it, 3))
-            if chunk_at(it, 4) >= 0:
-                epi_sh(chunk_at(it, 4))
-            if chunk_at(it, 6) >= 0:
-                epi_out(chunk_at(it, 6))
-            if 0 <= it - 1 < N_UNITS:
                 stage_e(it - 1)
+            when(it, 5, epi_exp)
+            when(it, 8, epi_out)
+            if M_ENGINE == "gpsimd":
+                when(it, 6, epi_m)
+            when(it, 6, epi_z1)
+            when(it, 4, epi_a1)
+            when(it, 4, epi_sh)
+            when(it, 6, epi_sum)
         nc.sync.dma_start(out=out_1.rearrange("(p i) -> p i", i=ROWS_PP), in_=ld[:])

@@ -25,7 +25,7 @@ FLOPS = 2 * 2 * B * HID * (HID + D_OUT)
 PIN = True
 H_ON_V = ()
 G_ON_V = ()
-Z1_ENGINE = "gpsimd"
+Z1_GP_ROWS = 2
 M_ENGINE = "gpsimd"
 
 
@@ -255,12 +255,14 @@ def tile_affinecouplinglayer_pa_t_kernel(
         def epi_z1(c):
             ot = epi.tile([P, CH, DIM], F32, name="ot")
             ot_t[c] = ot
-            if Z1_ENGINE == "gpsimd":
+            zr = z_rows(c, 0)
+            if Z1_GP_ROWS > 0:
                 nc.gpsimd.tensor_scalar(
-                    out=ot[:, :, 0:D_OUT], in0=z_rows(c, 0), scalar1=1.0, scalar2=0.0, op0=ALU.mult, op1=ALU.add
+                    out=ot[:, 0:Z1_GP_ROWS, 0:D_OUT], in0=zr[:, 0:Z1_GP_ROWS, :], scalar1=1.0, scalar2=0.0,
+                    op0=ALU.mult, op1=ALU.add,
                 )
-            else:
-                nc.scalar.copy(out=ot[:, :, 0:D_OUT], in_=z_rows(c, 0))
+            if Z1_GP_ROWS < CH:
+                nc.scalar.copy(out=ot[:, Z1_GP_ROWS:CH, 0:D_OUT], in_=zr[:, Z1_GP_ROWS:CH, :])
 
         def epi_exp(c):
             ex = epi.tile([P, CH, D_OUT], F32, name="ex")

@@ -114,13 +114,27 @@ def tile_affinecouplinglayer_pa_t_kernel(
             else:
                 nc.scalar.copy(out=out, in_=in_)
 
-        def to_k_major(words, first_word, grouped, prologue=False):
+        def to_k_major(words, first_word, grouped, prologue=False, warm=False):
             gw = grouped[:].bitcast(F32)
+            banks = []
             for half in range(2):
                 if prologue:
                     bank = m1_pool.tile([P, 2, 256], F32, name="m1")
                 else:
                     bank = tp_pool.tile([P, 2, 256], F32, name="tp")
+                banks.append(bank)
+                if warm:
+                    nc.tensor.matmul_mx(
+                        out=bank[:].rearrange("p u b -> p (u b)"),
+                        lhsT=wc[0][:, 0:P].bitcast(FP8X4),
+                        lhsT_scale=wsc[0][:, 0:P],
+                        rhs=wc[1][:].bitcast(FP8X4),
+                        rhs_scale=wsc[1][:],
+                        start=True,
+                        stop=True,
+                    )
+            for half in range(2):
+                bank = banks[half]
                 for r2 in range(2):
                     for uu in range(2):
                         w0 = first_word + (2 * half + r2) * 256 + uu * P
@@ -172,7 +186,7 @@ def tile_affinecouplinglayer_pa_t_kernel(
             c, n = u // 2, u % 2
             t = work.tile([P, 4 * HID], BF16, name="hq", align_bytes=64)
             hq[u] = t
-            to_k_major(h_sb[(n, c // 2)][:].bitcast(F32), (c % 2) * CH * 256, t)
+            to_k_major(h_sb[(n, c // 2)][:].bitcast(F32), (c % 2) * CH * 256, t, False, u >= 3)
 
         def stage_b(u):
             c = work.tile([P, HID], U32, name="hc", align_bytes=64)

@@ -25,8 +25,8 @@ FLOPS = 2 * 2 * B * HID * (HID + D_OUT)
 PIN = True
 H_ON_V = ()
 G_ON_V = ()
-Z1_GP_ROWS = 2
-M_ENGINE = "gpsimd"
+Z1_ENGINE = "scalar"
+M_ENGINE = "vector"
 
 
 def tile_affinecouplinglayer_pa_t_kernel(
@@ -114,27 +114,13 @@ def tile_affinecouplinglayer_pa_t_kernel(
             else:
                 nc.scalar.copy(out=out, in_=in_)
 
-        def to_k_major(words, first_word, grouped, prologue=False, warm=False):
+        def to_k_major(words, first_word, grouped, prologue=False):
             gw = grouped[:].bitcast(F32)
-            banks = []
             for half in range(2):
                 if prologue:
                     bank = m1_pool.tile([P, 2, 256], F32, name="m1")
                 else:
                     bank = tp_pool.tile([P, 2, 256], F32, name="tp")
-                banks.append(bank)
-                if warm:
-                    nc.tensor.matmul_mx(
-                        out=bank[:].rearrange("p u b -> p (u b)"),
-                        lhsT=wc[0][:, 0:P].bitcast(FP8X4),
-                        lhsT_scale=wsc[0][:, 0:P],
-                        rhs=wc[1][:].bitcast(FP8X4),
-                        rhs_scale=wsc[1][:],
-                        start=True,
-                        stop=True,
-                    )
-            for half in range(2):
-                bank = banks[half]
                 for r2 in range(2):
                     for uu in range(2):
                         w0 = first_word + (2 * half + r2) * 256 + uu * P
@@ -186,7 +172,7 @@ def tile_affinecouplinglayer_pa_t_kernel(
             c, n = u // 2, u % 2
             t = work.tile([P, 4 * HID], BF16, name="hq", align_bytes=64)
             hq[u] = t
-            to_k_major(h_sb[(n, c // 2)][:].bitcast(F32), (c % 2) * CH * 256, t, False, u >= 3)
+            to_k_major(h_sb[(n, c // 2)][:].bitcast(F32), (c % 2) * CH * 256, t)
 
         def stage_b(u):
             c = work.tile([P, HID], U32, name="hc", align_bytes=64)
@@ -269,14 +255,12 @@ def tile_affinecouplinglayer_pa_t_kernel(
         def epi_z1(c):
             ot = epi.tile([P, CH, DIM], F32, name="ot")
             ot_t[c] = ot
-            zr = z_rows(c, 0)
-            if Z1_GP_ROWS > 0:
+            if Z1_ENGINE == "gpsimd":
                 nc.gpsimd.tensor_scalar(
-                    out=ot[:, 0:Z1_GP_ROWS, 0:D_OUT], in0=zr[:, 0:Z1_GP_ROWS, :], scalar1=1.0, scalar2=0.0,
-                    op0=ALU.mult, op1=ALU.add,
+                    out=ot[:, :, 0:D_OUT], in0=z_rows(c, 0), scalar1=1.0, scalar2=0.0, op0=ALU.mult, op1=ALU.add
                 )
-            if Z1_GP_ROWS < CH:
-                nc.scalar.copy(out=ot[:, Z1_GP_ROWS:CH, 0:D_OUT], in_=zr[:, Z1_GP_ROWS:CH, :])
+            else:
+                nc.scalar.copy(out=ot[:, :, 0:D_OUT], in_=z_rows(c, 0))
 
         def epi_exp(c):
             ex = epi.tile([P, CH, D_OUT], F32, name="ex")

@@ -14,19 +14,16 @@ AX = mybir.AxisListType
 
 P = 128
 B, DIM, HID, D_OUT = 8192, 256, 512, 128
+PACK = 4
 ROWS_PP = B // P
-CH = 4
-SC = 8
-N_CHUNKS = ROWS_PP // CH
+TILES = 4
+COLS = TILES * P
+LOAD_TILES = 8
+N_CHUNKS = ROWS_PP // TILES
 N_UNITS = 2 * N_CHUNKS
-N_SC = ROWS_PP // SC
+N_LOADS = ROWS_PP // LOAD_TILES
+WORDS = HID // 2
 FLOPS = 2 * 2 * B * HID * (HID + D_OUT)
-
-PIN = True
-H_ON_V = ()
-G_ON_V = ()
-Z1_ENGINE = "scalar"
-M_ENGINE = "vector"
 
 
 def tile_affinecouplinglayer_pa_t_kernel(
@@ -35,7 +32,7 @@ def tile_affinecouplinglayer_pa_t_kernel(
     nc = tc.nc
     h_in = (h_s.rearrange("(p i) k -> p i k", i=ROWS_PP), h_t.rearrange("(p i) k -> p i k", i=ROWS_PP))
     z_in = z.rearrange("(p i) d -> p i d", i=ROWS_PP)
-    zo = out_0.rearrange("(p i) d -> p i d", i=ROWS_PP)
+    z_out = out_0.rearrange("(p i) d -> p i d", i=ROWS_PP)
     w_hid = (s_Whid1, t_Whid1)
     b_hid = (s_bhid1, t_bhid1)
     w_out = (s_Wout, t_Wout)
@@ -45,47 +42,44 @@ def tile_affinecouplinglayer_pa_t_kernel(
         const = ctx.enter_context(tc.tile_pool(name="const", bufs=1))
         hpool = ctx.enter_context(tc.tile_pool(name="hpool", bufs=3))
         zpool = ctx.enter_context(tc.tile_pool(name="zpool", bufs=5))
+        ring2 = ctx.enter_context(tc.tile_pool(name="ring2", bufs=2))
+        ring3 = ctx.enter_context(tc.tile_pool(name="ring3", bufs=3))
+        ring4 = ctx.enter_context(tc.tile_pool(name="ring4", bufs=4))
         gate = ctx.enter_context(tc.tile_pool(name="gate", bufs=1))
-        work = ctx.enter_context(tc.tile_pool(name="work", bufs=4))
-        epi = ctx.enter_context(tc.tile_pool(name="epi", bufs=4))
         tp_pool = ctx.enter_context(tc.psum_pool(name="tp_pool", bufs=2))
         m1_pool = ctx.enter_context(tc.psum_pool(name="m1_pool", bufs=4))
         m2_pool = ctx.enter_context(tc.psum_pool(name="m2_pool", bufs=2))
-        if PIN:
-            ctx.enter_context(tc.manual_schedule())
+        ctx.enter_context(tc.manual_schedule())
 
-        w_sb = []
-        wo_sb = []
-        bh_raw = []
-        bo_raw = []
-        h_sb = {}
-        z_sb = {}
+        h_sb, z_sb = {}, {}
+        w_sb, wo_sb, bh_raw, bo_raw = [], [], [], []
 
         def load_h_rows(n, s, i0, i1):
             nc.sync.dma_start(
                 out=h_sb[(n, s)][:, i0 * HID : i1 * HID].rearrange("p (i k) -> p i k", k=HID),
-                in_=h_in[n][:, s * SC + i0 : s * SC + i1, :],
+                in_=h_in[n][:, s * LOAD_TILES + i0 : s * LOAD_TILES + i1, :],
             )
 
-        def load_h(n, s):
-            t = hpool.tile([P, SC * HID], BF16, name="h%d" % n)
+        def new_h(n, s):
+            t = hpool.tile([P, LOAD_TILES * HID], BF16, name="h%d" % n)
             h_sb[(n, s)] = t
-            load_h_rows(n, s, 0, SC)
 
-        def load_z(s):
-            t = zpool.tile([P, SC, DIM], BF16, name="zt")
+        def load(s):
+            for n in range(2):
+                new_h(n, s)
+                load_h_rows(n, s, 0, LOAD_TILES)
+            t = zpool.tile([P, LOAD_TILES, DIM], BF16, name="zt")
             z_sb[s] = t
-            nc.sync.dma_start(out=t[:], in_=z_in[:, s * SC : (s + 1) * SC, :])
+            nc.sync.dma_start(out=t[:], in_=z_in[:, s * LOAD_TILES : (s + 1) * LOAD_TILES, :])
 
         for n in range(2):
-            wt = const.tile([P, 4 * HID], BF16, name="w_sb%d" % n)
-            nc.sync.dma_start(out=wt[:], in_=w_hid[n].rearrange("(p t) k -> p (t k)", t=4))
+            wt = const.tile([P, PACK * HID], BF16, name="w_sb%d" % n)
+            nc.sync.dma_start(out=wt[:], in_=w_hid[n].rearrange("(p t) k -> p (t k)", t=PACK))
             w_sb.append(wt)
-            h0 = hpool.tile([P, SC * HID], BF16, name="h%d" % n)
-            h_sb[(n, 0)] = h0
-            load_h_rows(n, 0, 0, CH)
-            br = const.tile([P, 4], BF16, name="bh_raw%d" % n)
-            nc.scalar.dma_start(out=br[:], in_=b_hid[n].rearrange("(p t) -> p t", t=4))
+            new_h(n, 0)
+            load_h_rows(n, 0, 0, TILES)
+            br = const.tile([P, PACK], BF16, name="bh_raw%d" % n)
+            nc.scalar.dma_start(out=br[:], in_=b_hid[n].rearrange("(p t) -> p t", t=PACK))
             bh_raw.append(br)
             wo = const.tile([P, HID], BF16, name="wo_sb%d" % n)
             nc.scalar.dma_start(out=wo[:], in_=w_out[n])
@@ -95,61 +89,52 @@ def tile_affinecouplinglayer_pa_t_kernel(
             nc.scalar.dma_start(out=bo[:], in_=b_out[n].partition_broadcast(P))
             bo_raw.append(bo)
         for n in range(2):
-            load_h_rows(n, 0, CH, SC)
-        load_z(0)
-        for n in range(2):
-            load_h(n, 1)
-        load_z(1)
+            load_h_rows(n, 0, TILES, LOAD_TILES)
+        z0 = zpool.tile([P, LOAD_TILES, DIM], BF16, name="zt")
+        z_sb[0] = z0
+        nc.sync.dma_start(out=z0[:], in_=z_in[:, 0:LOAD_TILES, :])
+        load(1)
 
         ident = const.tile([P, P], F32, name="ident")
         make_identity(nc, ident[:])
 
-        counters = {"h": 0, "g": 0}
-
-        def copy_out(out, in_, on_vector):
-            i = counters["h"] % 4
-            counters["h"] += 1
-            if on_vector or i in H_ON_V:
-                nc.vector.tensor_copy(out=out, in_=in_)
-            else:
-                nc.scalar.copy(out=out, in_=in_)
-
-        def to_k_major(words, first_word, grouped, prologue=False):
-            gw = grouped[:].bitcast(F32)
+        def to_k_major(words, first_word, grouped_words, weights):
             for half in range(2):
-                if prologue:
-                    bank = m1_pool.tile([P, 2, 256], F32, name="m1")
+                if weights:
+                    bank = m1_pool.tile([P, 2, 2 * P], F32, name="m1")
                 else:
-                    bank = tp_pool.tile([P, 2, 256], F32, name="tp")
-                for r2 in range(2):
-                    for uu in range(2):
-                        w0 = first_word + (2 * half + r2) * 256 + uu * P
-                        nc.tensor.transpose(bank[:, uu, r2 * P : (r2 + 1) * P], words[:, w0 : w0 + P], ident[:])
-                copy_out(
-                    gw[:, half * 512 : (half + 1) * 512].rearrange("p (b u) -> p b u", u=2),
-                    bank[:].rearrange("p u b -> p b u"),
-                    prologue,
-                )
+                    bank = tp_pool.tile([P, 2, 2 * P], F32, name="tp")
+                for r in range(2):
+                    for u in range(2):
+                        w0 = first_word + (2 * half + r) * WORDS + u * P
+                        nc.tensor.transpose(bank[:, u, r * P : (r + 1) * P], words[:, w0 : w0 + P], ident[:])
+                dst = grouped_words[:, half * 4 * P : (half + 1) * 4 * P].rearrange("p (b u) -> p b u", u=2)
+                src = bank[:].rearrange("p u b -> p b u")
+                if weights:
+                    nc.vector.tensor_copy(out=dst, in_=src)
+                else:
+                    nc.scalar.copy(out=dst, in_=src)
 
         wc, wsc, woc, wosc, bh, bo = [], [], [], [], [], []
+
         def prep_w(n):
-            wq = work.tile([P, 4 * HID], BF16, name="hq", align_bytes=64)
-            to_k_major(w_sb[n][:].bitcast(F32), 0, wq, True)
+            wq = const.tile([P, PACK * HID], BF16, name="wq%d" % n, align_bytes=64)
+            to_k_major(w_sb[n][:].bitcast(F32), 0, wq[:].bitcast(F32), True)
             c = const.tile([P, HID], U32, name="wc%d" % n, align_bytes=64)
             s = const.tile([P, HID], U8, name="wsc%d" % n, align_bytes=64)
             nc.vector.quantize_mx(out=c[:].bitcast(FP8X4), scales=s[:], in_=wq[:])
             wc.append(c)
             wsc.append(s)
-            b32 = const.tile([P, 4], F32, name="bh%d" % n)
+            b32 = const.tile([P, PACK], F32, name="bh%d" % n)
             nc.vector.tensor_copy(out=b32[:], in_=bh_raw[n][:])
             bh.append(b32)
 
         def prep_wout(n):
-            bank = m2_pool.tile([P, 2, 256], F32, name="m2")
+            bank = m2_pool.tile([P, 2, 2 * P], F32, name="m2")
             wv = wo_sb[n][:].bitcast(F32).rearrange("p (q u) -> p u q", u=2)
-            for uu in range(2):
-                nc.tensor.transpose(bank[:, uu, 0:P], wv[:, uu, :], ident[:])
-            woq = const.tile([P, 4 * D_OUT], BF16, name="woq%d" % n, align_bytes=64)
+            for u in range(2):
+                nc.tensor.transpose(bank[:, u, 0:P], wv[:, u, :], ident[:])
+            woq = const.tile([P, PACK * D_OUT], BF16, name="woq%d" % n, align_bytes=64)
             nc.vector.tensor_copy(
                 out=woq[:].bitcast(F32).rearrange("p (b u) -> p b u", u=2),
                 in_=bank[:, :, 0:P].rearrange("p u b -> p b u"),
@@ -163,174 +148,172 @@ def tile_affinecouplinglayer_pa_t_kernel(
             nc.vector.tensor_copy(out=b32[:], in_=bo_raw[n][:])
             bo.append(b32)
 
-        ld = const.tile([P, ROWS_PP], F32, name="ld")
+        log_det = const.tile([P, ROWS_PP], F32, name="log_det")
 
         hq, hc, hsc, gt, gg, gc, gsc, o_ps = {}, {}, {}, {}, {}, {}, {}, {}
         ls_t, ex_t, ot_t, sh_t, mz_t = {}, {}, {}, {}, {}
 
-        def stage_a(u):
+        def transpose_h(u):
             c, n = u // 2, u % 2
-            t = work.tile([P, 4 * HID], BF16, name="hq", align_bytes=64)
-            hq[u] = t
-            to_k_major(h_sb[(n, c // 2)][:].bitcast(F32), (c % 2) * CH * 256, t)
+            if n == 0:
+                t = ring3.tile([P, 2 * PACK * COLS], BF16, name="hq", align_bytes=64)
+                hq[c] = t
+            to_k_major(
+                h_sb[(n, c // 2)][:].bitcast(F32),
+                (c % 2) * TILES * WORDS,
+                hq[c][:].bitcast(F32)[:, n * 2 * COLS : (n + 1) * 2 * COLS],
+                False,
+            )
 
-        def stage_b(u):
-            c = work.tile([P, HID], U32, name="hc", align_bytes=64)
-            s = work.tile([P, HID], U8, name="hsc", align_bytes=64)
-            nc.vector.quantize_mx(out=c[:].bitcast(FP8X4), scales=s[:], in_=hq[u][:])
-            hc[u], hsc[u] = c, s
+        def quantise_h(c, n0, n1):
+            if n0 == 0:
+                cw = ring3.tile([P, 2 * COLS], U32, name="hc", align_bytes=64)
+                sw = ring3.tile([P, 2 * COLS], U8, name="hsc", align_bytes=64)
+                hc[c], hsc[c] = cw, sw
+            nc.vector.quantize_mx(
+                out=hc[c][:, n0 * COLS : n1 * COLS].bitcast(FP8X4),
+                scales=hsc[c][:, n0 * COLS : n1 * COLS],
+                in_=hq[c][:, n0 * PACK * COLS : n1 * PACK * COLS],
+            )
 
-        def stage_c(u):
-            n = u % 2
-            g = work.tile([P, 4, 512], BF16, name="gt")
-            gt[u] = g
-            for t in range(4):
-                acc = m1_pool.tile([P, 512], F32, name="m1")
+        def hidden_layer(u):
+            c, n = u // 2, u % 2
+            if n == 0:
+                g = ring3.tile([P, PACK, 2 * COLS], BF16, name="gt")
+                gt[c] = g
+            cols = slice(n * COLS, (n + 1) * COLS)
+            for t in range(PACK):
+                acc = m1_pool.tile([P, COLS], F32, name="m1")
                 nc.tensor.matmul_mx(
                     out=acc[:],
                     lhsT=wc[n][:, t * P : (t + 1) * P].bitcast(FP8X4),
                     lhsT_scale=wsc[n][:, t * P : (t + 1) * P],
-                    rhs=hc[u][:].bitcast(FP8X4),
-                    rhs_scale=hsc[u][:],
+                    rhs=hc[c][:, cols].bitcast(FP8X4),
+                    rhs_scale=hsc[c][:, cols],
                     start=True,
                     stop=True,
                 )
-                i = counters["g"] % 8
-                counters["g"] += 1
-                if i in G_ON_V:
-                    nc.vector.tensor_scalar(
-                        out=g[:, t, :], in0=acc[:], scalar1=bh[n][:, t : t + 1], scalar2=0.0, op0=ALU.add, op1=ALU.max
-                    )
-                else:
-                    nc.scalar.activation(out=g[:, t, :], in_=acc[:], func=ACT.Relu, bias=bh[n][:, t : t + 1], scale=1.0)
+                nc.scalar.activation(out=gt[c][:, t, cols], in_=acc[:], func=ACT.Relu, bias=bh[n][:, t : t + 1], scale=1.0)
 
-        def stage_d(u):
-            t = work.tile([P, 512, 4], BF16, name="gg", align_bytes=64)
-            gg[u] = t
+        def regroup_g(c):
+            t = ring2.tile([P, 2 * COLS, PACK], BF16, name="gg", align_bytes=64)
+            gg[c] = t
             nc.vector.tensor_copy(
                 out=t[:].rearrange("p (c i) t -> p c t i", i=4),
-                in_=gt[u][:].rearrange("p t (c i) -> p c t i", i=4),
+                in_=gt[c][:].rearrange("p t (c i) -> p c t i", i=4),
             )
 
-        def stage_e(u):
-            c = work.tile([P, HID], U32, name="gc", align_bytes=64)
-            s = work.tile([P, HID], U8, name="gsc", align_bytes=64)
-            nc.vector.quantize_mx(out=c[:].bitcast(FP8X4), scales=s[:], in_=gg[u][:].rearrange("p b t -> p (b t)"))
-            gc[u], gsc[u] = c, s
+        def quantise_g(c):
+            cw = ring2.tile([P, 2 * COLS], U32, name="gc", align_bytes=64)
+            sw = ring2.tile([P, 2 * COLS], U8, name="gsc", align_bytes=64)
+            nc.vector.quantize_mx(out=cw[:].bitcast(FP8X4), scales=sw[:], in_=gg[c][:].rearrange("p b t -> p (b t)"))
+            gc[c], gsc[c] = cw, sw
 
-        def stage_f(u):
-            n = u % 2
-            o = m2_pool.tile([P, CH, D_OUT], F32, name="m2")
-            o_ps[u] = o
-            for r in range(CH):
-                nc.tensor.matmul_mx(
-                    out=o[:, r, :],
-                    lhsT=gc[u][:, r * P : (r + 1) * P].bitcast(FP8X4),
-                    lhsT_scale=gsc[u][:, r * P : (r + 1) * P],
-                    rhs=woc[n][:].bitcast(FP8X4),
-                    rhs_scale=wosc[n][:],
-                    start=True,
-                    stop=True,
-                )
+        def output_layer(c):
+            for n in range(2):
+                o = m2_pool.tile([P, TILES, D_OUT], F32, name="m2")
+                o_ps[(c, n)] = o
+                for r in range(TILES):
+                    cols = slice(n * COLS + r * P, n * COLS + (r + 1) * P)
+                    nc.tensor.matmul_mx(
+                        out=o[:, r, :],
+                        lhsT=gc[c][:, cols].bitcast(FP8X4),
+                        lhsT_scale=gsc[c][:, cols],
+                        rhs=woc[n][:].bitcast(FP8X4),
+                        rhs_scale=wosc[n][:],
+                        start=True,
+                        stop=True,
+                    )
 
         def bias_rows(n):
-            return bo[n][:].unsqueeze(1).to_broadcast([P, CH, D_OUT])
+            return bo[n][:].unsqueeze(1).to_broadcast([P, TILES, D_OUT])
 
         def z_rows(c, lo):
-            i0 = (c % 2) * CH
-            return z_sb[c // 2][:, i0 : i0 + CH, lo : lo + D_OUT]
+            i0 = (c % 2) * TILES
+            return z_sb[c // 2][:, i0 : i0 + TILES, lo : lo + D_OUT]
 
-        def epi_a1(c):
-            ls = epi.tile([P, CH, D_OUT], F32, name="ls")
+        def add_scale_bias(c):
+            ls = ring3.tile([P, TILES, D_OUT], F32, name="ls")
             ls_t[c] = ls
-            nc.vector.tensor_tensor(out=ls[:], in0=o_ps[2 * c][:], in1=bias_rows(0), op=ALU.add)
+            nc.vector.tensor_tensor(out=ls[:], in0=o_ps[(c, 0)][:], in1=bias_rows(0), op=ALU.add)
 
-        def epi_clamp(c):
+        def add_shift_bias(c):
+            sh = ring3.tile([P, TILES, D_OUT], F32, name="sh")
+            sh_t[c] = sh
+            nc.vector.tensor_tensor(out=sh[:], in0=o_ps[(c, 1)][:], in1=bias_rows(1), op=ALU.add)
+
+        def clamp(c):
             ls = ls_t[c]
             nc.vector.tensor_scalar(out=ls[:], in0=ls[:], scalar1=-2.0, scalar2=2.0, op0=ALU.max, op1=ALU.min)
 
-        def epi_sum(c):
-            nc.vector.tensor_reduce(out=ld[:, c * CH : (c + 1) * CH], in_=ls_t[c][:], axis=AX.X, op=ALU.add)
-
-        def epi_z1(c):
-            ot = epi.tile([P, CH, DIM], F32, name="ot")
-            ot_t[c] = ot
-            if Z1_ENGINE == "gpsimd":
-                nc.gpsimd.tensor_scalar(
-                    out=ot[:, :, 0:D_OUT], in0=z_rows(c, 0), scalar1=1.0, scalar2=0.0, op0=ALU.mult, op1=ALU.add
-                )
-            else:
-                nc.scalar.copy(out=ot[:, :, 0:D_OUT], in_=z_rows(c, 0))
-
-        def epi_exp(c):
-            ex = epi.tile([P, CH, D_OUT], F32, name="ex")
+        def exponential(c):
+            ex = ring2.tile([P, TILES, D_OUT], F32, name="ex")
             ex_t[c] = ex
             nc.scalar.activation(out=ex[:], in_=ls_t[c][:], func=ACT.Exp)
 
-        def epi_sh(c):
-            sh = epi.tile([P, CH, D_OUT], F32, name="sh")
-            sh_t[c] = sh
-            nc.vector.tensor_tensor(out=sh[:], in0=o_ps[2 * c + 1][:], in1=bias_rows(1), op=ALU.add)
+        def row_sums(c):
+            nc.vector.tensor_reduce(out=log_det[:, c * TILES : (c + 1) * TILES], in_=ls_t[c][:], axis=AX.X, op=ALU.add)
 
-        def epi_m(c):
-            mz = gate.tile([P, CH, D_OUT], F32, name="mz")
+        def scale_z2(c):
+            mz = gate.tile([P, TILES, D_OUT], F32, name="mz")
             mz_t[c] = mz
-            eng = nc.gpsimd if M_ENGINE == "gpsimd" else nc.vector
-            eng.tensor_tensor(out=mz[:], in0=z_rows(c, D_OUT), in1=ex_t[c][:], op=ALU.mult)
+            nc.gpsimd.tensor_tensor(out=mz[:], in0=z_rows(c, D_OUT), in1=ex_t[c][:], op=ALU.mult)
 
-        def epi_out(c):
+        def cast_z1_first_half(c):
+            ot = ring4.tile([P, TILES, DIM], F32, name="ot")
+            ot_t[c] = ot
+            nc.gpsimd.tensor_scalar(
+                out=ot[:, 0 : TILES // 2, 0:D_OUT],
+                in0=z_rows(c, 0)[:, 0 : TILES // 2, :],
+                scalar1=1.0,
+                scalar2=0.0,
+                op0=ALU.mult,
+                op1=ALU.add,
+            )
+
+        def cast_z1_second_half(c):
+            nc.scalar.copy(out=ot_t[c][:, TILES // 2 : TILES, 0:D_OUT], in_=z_rows(c, 0)[:, TILES // 2 : TILES, :])
+
+        def finish(c):
             nc.vector.tensor_tensor(out=ot_t[c][:, :, D_OUT:DIM], in0=mz_t[c][:], in1=sh_t[c][:], op=ALU.add)
-            nc.sync.dma_start(out=zo[:, c * CH : (c + 1) * CH, :], in_=ot_t[c][:])
-
-        prep_w(0)
-        stage_a(0)
-        stage_b(0)
-        prep_w(1)
-        stage_a(1)
-        stage_a(2)
-
-        def chunk_at(it, first):
-            c = (it - first) // 2
-            return c if (it >= first and (it - first) % 2 == 0 and c < N_CHUNKS) else -1
+            nc.sync.dma_start(out=z_out[:, c * TILES : (c + 1) * TILES, :], in_=ot_t[c][:])
 
         def when(it, first, fn):
-            c = chunk_at(it, first)
-            if c >= 0:
+            c = (it - first) // 2
+            if it >= first and (it - first) % 2 == 0 and c < N_CHUNKS:
                 fn(c)
 
-        for it in range(N_UNITS + 7):
+        prep_w(0)
+        transpose_h(0)
+        quantise_h(0, 0, 1)
+        prep_w(1)
+        transpose_h(1)
+
+        for it in range(N_UNITS + 8):
+            when(it, 7, exponential)
             if it < N_UNITS:
-                stage_c(it)
+                hidden_layer(it)
             if it == 0:
                 prep_wout(0)
                 prep_wout(1)
+                transpose_h(2)
             if it + 3 < N_UNITS:
-                if (it + 3) % 4 == 0:
-                    s_next = (it + 3) // 4 + 1
-                    if s_next < N_SC:
-                        for n in range(2):
-                            load_h(n, s_next)
-                        load_z(s_next)
-                stage_a(it + 3)
-            c_f = chunk_at(it, 3)
-            if c_f >= 0:
-                stage_f(2 * c_f)
-                stage_f(2 * c_f + 1)
-            if 0 <= it - 1 < N_UNITS:
-                stage_d(it - 1)
-            when(it, 5, epi_clamp)
-            if M_ENGINE != "gpsimd":
-                when(it, 7, epi_m)
-            if it + 1 < N_UNITS:
-                stage_b(it + 1)
-            if 0 <= it - 1 < N_UNITS:
-                stage_e(it - 1)
-            when(it, 5, epi_exp)
-            when(it, 8, epi_out)
-            if M_ENGINE == "gpsimd":
-                when(it, 6, epi_m)
-            when(it, 6, epi_z1)
-            when(it, 4, epi_a1)
-            when(it, 4, epi_sh)
-            when(it, 6, epi_sum)
-        nc.sync.dma_start(out=out_1.rearrange("(p i) -> p i", i=ROWS_PP), in_=ld[:])
+                if (it + 3) % 4 == 0 and (it + 3) // 4 + 1 < N_LOADS:
+                    load((it + 3) // 4 + 1)
+                transpose_h(it + 3)
+            when(it, 4, output_layer)
+            when(it, 8, cast_z1_second_half)
+            if it == 0:
+                quantise_h(0, 1, 2)
+            if it % 2 == 1 and (it + 1) // 2 < N_CHUNKS:
+                quantise_h((it + 1) // 2, 0, 2)
+            when(it, 9, finish)
+            when(it, 7, scale_z2)
+            when(it, 7, cast_z1_first_half)
+            when(it, 5, add_scale_bias)
+            when(it, 5, add_shift_bias)
+            when(it, 7, row_sums)
+            when(it, 2, regroup_g)
+            when(it, 6, clamp)
+            when(it, 2, quantise_g)
+        nc.sync.dma_start(out=out_1.rearrange("(p i) -> p i", i=ROWS_PP), in_=log_det[:])

from contextlib import ExitStack

import concourse.mybir as mybir
from concourse.masks import make_identity

F32 = mybir.dt.float32
BF16 = mybir.dt.bfloat16
U32 = mybir.dt.uint32
U8 = mybir.dt.uint8
FP8X4 = mybir.dt.float8_e4m3fn_x4
ACT = mybir.ActivationFunctionType
ALU = mybir.AluOpType
AX = mybir.AxisListType

P = 128
B, DIM, HID, D_OUT = 8192, 256, 512, 128
PACK = 4
ROWS_PP = B // P
TILES = 4
COLS = TILES * P
LOAD_TILES = 8
N_CHUNKS = ROWS_PP // TILES
N_UNITS = 2 * N_CHUNKS
N_LOADS = ROWS_PP // LOAD_TILES
WORDS = HID // 2
FLOPS = 2 * 2 * B * HID * (HID + D_OUT)


def tile_affinecouplinglayer_pa_t_kernel(
    tc, z, h_s, h_t, s_Whid1, s_bhid1, s_Wout, s_bout, t_Whid1, t_bhid1, t_Wout, t_bout, out_0, out_1
):
    nc = tc.nc
    h_in = (h_s.rearrange("(p i) k -> p i k", i=ROWS_PP), h_t.rearrange("(p i) k -> p i k", i=ROWS_PP))
    z_in = z.rearrange("(p i) d -> p i d", i=ROWS_PP)
    z_out = out_0.rearrange("(p i) d -> p i d", i=ROWS_PP)
    w_hid = (s_Whid1, t_Whid1)
    b_hid = (s_bhid1, t_bhid1)
    w_out = (s_Wout, t_Wout)
    b_out = (s_bout, t_bout)

    with ExitStack() as ctx:
        const = ctx.enter_context(tc.tile_pool(name="const", bufs=1))
        hpool = ctx.enter_context(tc.tile_pool(name="hpool", bufs=3))
        zpool = ctx.enter_context(tc.tile_pool(name="zpool", bufs=5))
        ring2 = ctx.enter_context(tc.tile_pool(name="ring2", bufs=2))
        ring3 = ctx.enter_context(tc.tile_pool(name="ring3", bufs=3))
        ring4 = ctx.enter_context(tc.tile_pool(name="ring4", bufs=4))
        gate = ctx.enter_context(tc.tile_pool(name="gate", bufs=1))
        tp_pool = ctx.enter_context(tc.psum_pool(name="tp_pool", bufs=2))
        m1_pool = ctx.enter_context(tc.psum_pool(name="m1_pool", bufs=4))
        m2_pool = ctx.enter_context(tc.psum_pool(name="m2_pool", bufs=2))
        ctx.enter_context(tc.manual_schedule())

        h_sb, z_sb = {}, {}
        w_sb, wo_sb, bh_raw, bo_raw = [], [], [], []

        def load_h_rows(n, s, i0, i1):
            nc.sync.dma_start(
                out=h_sb[(n, s)][:, i0 * HID : i1 * HID].rearrange("p (i k) -> p i k", k=HID),
                in_=h_in[n][:, s * LOAD_TILES + i0 : s * LOAD_TILES + i1, :],
            )

        def new_h(n, s):
            t = hpool.tile([P, LOAD_TILES * HID], BF16, name="h%d" % n)
            h_sb[(n, s)] = t

        def load(s):
            for n in range(2):
                new_h(n, s)
                load_h_rows(n, s, 0, LOAD_TILES)
            t = zpool.tile([P, LOAD_TILES, DIM], BF16, name="zt")
            z_sb[s] = t
            nc.sync.dma_start(out=t[:], in_=z_in[:, s * LOAD_TILES : (s + 1) * LOAD_TILES, :])

        for n in range(2):
            wt = const.tile([P, PACK * HID], BF16, name="w_sb%d" % n)
            nc.sync.dma_start(out=wt[:], in_=w_hid[n].rearrange("(p t) k -> p (t k)", t=PACK))
            w_sb.append(wt)
            new_h(n, 0)
            load_h_rows(n, 0, 0, TILES)
            br = const.tile([P, PACK], BF16, name="bh_raw%d" % n)
            nc.scalar.dma_start(out=br[:], in_=b_hid[n].rearrange("(p t) -> p t", t=PACK))
            bh_raw.append(br)
            wo = const.tile([P, HID], BF16, name="wo_sb%d" % n)
            nc.scalar.dma_start(out=wo[:], in_=w_out[n])
            wo_sb.append(wo)
        for n in range(2):
            bo = const.tile([P, D_OUT], BF16, name="bo_raw%d" % n)
            nc.scalar.dma_start(out=bo[:], in_=b_out[n].partition_broadcast(P))
            bo_raw.append(bo)
        for n in range(2):
            load_h_rows(n, 0, TILES, LOAD_TILES)
        z0 = zpool.tile([P, LOAD_TILES, DIM], BF16, name="zt")
        z_sb[0] = z0
        nc.sync.dma_start(out=z0[:], in_=z_in[:, 0:LOAD_TILES, :])
        load(1)

        ident = const.tile([P, P], F32, name="ident")
        make_identity(nc, ident[:])

        def to_k_major(words, first_word, grouped_words, weights):
            for half in range(2):
                if weights:
                    bank = m1_pool.tile([P, 2, 2 * P], F32, name="m1")
                else:
                    bank = tp_pool.tile([P, 2, 2 * P], F32, name="tp")
                for r in range(2):
                    for u in range(2):
                        w0 = first_word + (2 * half + r) * WORDS + u * P
                        nc.tensor.transpose(bank[:, u, r * P : (r + 1) * P], words[:, w0 : w0 + P], ident[:])
                dst = grouped_words[:, half * 4 * P : (half + 1) * 4 * P].rearrange("p (b u) -> p b u", u=2)
                src = bank[:].rearrange("p u b -> p b u")
                if weights:
                    nc.vector.tensor_copy(out=dst, in_=src)
                else:
                    nc.scalar.copy(out=dst, in_=src)

        wc, wsc, woc, wosc, bh, bo = [], [], [], [], [], []

        def prep_w(n):
            wq = const.tile([P, PACK * HID], BF16, name="wq%d" % n, align_bytes=64)
            to_k_major(w_sb[n][:].bitcast(F32), 0, wq[:].bitcast(F32), True)
            c = const.tile([P, HID], U32, name="wc%d" % n, align_bytes=64)
            s = const.tile([P, HID], U8, name="wsc%d" % n, align_bytes=64)
            nc.vector.quantize_mx(out=c[:].bitcast(FP8X4), scales=s[:], in_=wq[:])
            wc.append(c)
            wsc.append(s)
            b32 = const.tile([P, PACK], F32, name="bh%d" % n)
            nc.vector.tensor_copy(out=b32[:], in_=bh_raw[n][:])
            bh.append(b32)

        def prep_wout(n):
            bank = m2_pool.tile([P, 2, 2 * P], F32, name="m2")
            wv = wo_sb[n][:].bitcast(F32).rearrange("p (q u) -> p u q", u=2)
            for u in range(2):
                nc.tensor.transpose(bank[:, u, 0:P], wv[:, u, :], ident[:])
            woq = const.tile([P, PACK * D_OUT], BF16, name="woq%d" % n, align_bytes=64)
            nc.vector.tensor_copy(
                out=woq[:].bitcast(F32).rearrange("p (b u) -> p b u", u=2),
                in_=bank[:, :, 0:P].rearrange("p u b -> p b u"),
            )
            c = const.tile([P, D_OUT], U32, name="woc%d" % n, align_bytes=64)
            s = const.tile([P, D_OUT], U8, name="wosc%d" % n, align_bytes=64)
            nc.vector.quantize_mx(out=c[:].bitcast(FP8X4), scales=s[:], in_=woq[:])
            woc.append(c)
            wosc.append(s)
            b32 = const.tile([P, D_OUT], F32, name="bo%d" % n)
            nc.vector.tensor_copy(out=b32[:], in_=bo_raw[n][:])
            bo.append(b32)

        log_det = const.tile([P, ROWS_PP], F32, name="log_det")

        hq, hc, hsc, gt, gg, gc, gsc, o_ps = {}, {}, {}, {}, {}, {}, {}, {}
        ls_t, ex_t, ot_t, sh_t, mz_t = {}, {}, {}, {}, {}

        def transpose_h(u):
            c, n = u // 2, u % 2
            if n == 0:
                t = ring3.tile([P, 2 * PACK * COLS], BF16, name="hq", align_bytes=64)
                hq[c] = t
            to_k_major(
                h_sb[(n, c // 2)][:].bitcast(F32),
                (c % 2) * TILES * WORDS,
                hq[c][:].bitcast(F32)[:, n * 2 * COLS : (n + 1) * 2 * COLS],
                False,
            )

        def quantise_h(c, n0, n1):
            if n0 == 0:
                cw = ring3.tile([P, 2 * COLS], U32, name="hc", align_bytes=64)
                sw = ring3.tile([P, 2 * COLS], U8, name="hsc", align_bytes=64)
                hc[c], hsc[c] = cw, sw
            nc.vector.quantize_mx(
                out=hc[c][:, n0 * COLS : n1 * COLS].bitcast(FP8X4),
                scales=hsc[c][:, n0 * COLS : n1 * COLS],
                in_=hq[c][:, n0 * PACK * COLS : n1 * PACK * COLS],
            )

        def hidden_layer(u):
            c, n = u // 2, u % 2
            if n == 0:
                g = ring3.tile([P, PACK, 2 * COLS], BF16, name="gt")
                gt[c] = g
            cols = slice(n * COLS, (n + 1) * COLS)
            for t in range(PACK):
                acc = m1_pool.tile([P, COLS], F32, name="m1")
                nc.tensor.matmul_mx(
                    out=acc[:],
                    lhsT=wc[n][:, t * P : (t + 1) * P].bitcast(FP8X4),
                    lhsT_scale=wsc[n][:, t * P : (t + 1) * P],
                    rhs=hc[c][:, cols].bitcast(FP8X4),
                    rhs_scale=hsc[c][:, cols],
                    start=True,
                    stop=True,
                )
                nc.scalar.activation(out=gt[c][:, t, cols], in_=acc[:], func=ACT.Relu, bias=bh[n][:, t : t + 1], scale=1.0)

        def regroup_g(c):
            t = ring2.tile([P, 2 * COLS, PACK], BF16, name="gg", align_bytes=64)
            gg[c] = t
            nc.vector.tensor_copy(
                out=t[:].rearrange("p (c i) t -> p c t i", i=4),
                in_=gt[c][:].rearrange("p t (c i) -> p c t i", i=4),
            )

        def quantise_g(c):
            cw = ring2.tile([P, 2 * COLS], U32, name="gc", align_bytes=64)
            sw = ring2.tile([P, 2 * COLS], U8, name="gsc", align_bytes=64)
            nc.vector.quantize_mx(out=cw[:].bitcast(FP8X4), scales=sw[:], in_=gg[c][:].rearrange("p b t -> p (b t)"))
            gc[c], gsc[c] = cw, sw

        def output_layer(c):
            for n in range(2):
                o = m2_pool.tile([P, TILES, D_OUT], F32, name="m2")
                o_ps[(c, n)] = o
                for r in range(TILES):
                    cols = slice(n * COLS + r * P, n * COLS + (r + 1) * P)
                    nc.tensor.matmul_mx(
                        out=o[:, r, :],
                        lhsT=gc[c][:, cols].bitcast(FP8X4),
                        lhsT_scale=gsc[c][:, cols],
                        rhs=woc[n][:].bitcast(FP8X4),
                        rhs_scale=wosc[n][:],
                        start=True,
                        stop=True,
                    )

        def bias_rows(n):
            return bo[n][:].unsqueeze(1).to_broadcast([P, TILES, D_OUT])

        def z_rows(c, lo):
            i0 = (c % 2) * TILES
            return z_sb[c // 2][:, i0 : i0 + TILES, lo : lo + D_OUT]

        def add_scale_bias(c):
            ls = ring3.tile([P, TILES, D_OUT], F32, name="ls")
            ls_t[c] = ls
            nc.vector.tensor_tensor(out=ls[:], in0=o_ps[(c, 0)][:], in1=bias_rows(0), op=ALU.add)

        def add_shift_bias(c):
            sh = ring3.tile([P, TILES, D_OUT], F32, name="sh")
            sh_t[c] = sh
            nc.vector.tensor_tensor(out=sh[:], in0=o_ps[(c, 1)][:], in1=bias_rows(1), op=ALU.add)

        def clamp(c):
            ls = ls_t[c]
            nc.vector.tensor_scalar(out=ls[:], in0=ls[:], scalar1=-2.0, scalar2=2.0, op0=ALU.max, op1=ALU.min)

        def exponential(c):
            ex = ring2.tile([P, TILES, D_OUT], F32, name="ex")
            ex_t[c] = ex
            nc.scalar.activation(out=ex[:], in_=ls_t[c][:], func=ACT.Exp)

        def row_sums(c):
            nc.vector.tensor_reduce(out=log_det[:, c * TILES : (c + 1) * TILES], in_=ls_t[c][:], axis=AX.X, op=ALU.add)

        def scale_z2(c):
            mz = gate.tile([P, TILES, D_OUT], F32, name="mz")
            mz_t[c] = mz
            nc.gpsimd.tensor_tensor(out=mz[:], in0=z_rows(c, D_OUT), in1=ex_t[c][:], op=ALU.mult)

        def cast_z1_first_half(c):
            ot = ring4.tile([P, TILES, DIM], F32, name="ot")
            ot_t[c] = ot
            nc.gpsimd.tensor_scalar(
                out=ot[:, 0 : TILES // 2, 0:D_OUT],
                in0=z_rows(c, 0)[:, 0 : TILES // 2, :],
                scalar1=1.0,
                scalar2=0.0,
                op0=ALU.mult,
                op1=ALU.add,
            )

        def cast_z1_second_half(c):
            nc.scalar.copy(out=ot_t[c][:, TILES // 2 : TILES, 0:D_OUT], in_=z_rows(c, 0)[:, TILES // 2 : TILES, :])

        def finish(c):
            nc.vector.tensor_tensor(out=ot_t[c][:, :, D_OUT:DIM], in0=mz_t[c][:], in1=sh_t[c][:], op=ALU.add)
            nc.sync.dma_start(out=z_out[:, c * TILES : (c + 1) * TILES, :], in_=ot_t[c][:])

        def when(it, first, fn):
            c = (it - first) // 2
            if it >= first and (it - first) % 2 == 0 and c < N_CHUNKS:
                fn(c)

        prep_w(0)
        transpose_h(0)
        quantise_h(0, 0, 1)
        prep_w(1)
        transpose_h(1)

        for it in range(N_UNITS + 8):
            when(it, 7, exponential)
            if it < N_UNITS:
                hidden_layer(it)
            if it == 0:
                prep_wout(0)
                prep_wout(1)
                transpose_h(2)
            if it + 3 < N_UNITS:
                if (it + 3) % 4 == 0 and (it + 3) // 4 + 1 < N_LOADS:
                    load((it + 3) // 4 + 1)
                transpose_h(it + 3)
            when(it, 4, output_layer)
            when(it, 8, cast_z1_second_half)
            if it == 0:
                quantise_h(0, 1, 2)
            if it % 2 == 1 and (it + 1) // 2 < N_CHUNKS:
                quantise_h((it + 1) // 2, 0, 2)
            when(it, 9, finish)
            when(it, 7, scale_z2)
            when(it, 7, cast_z1_first_half)
            when(it, 5, add_scale_bias)
            when(it, 5, add_shift_bias)
            when(it, 7, row_sums)
            when(it, 2, regroup_g)
            when(it, 6, clamp)
            when(it, 2, quantise_g)
        nc.sync.dma_start(out=out_1.rearrange("(p i) -> p i", i=ROWS_PP), in_=log_det[:])
